import numpy as np
import ml_dtypes


def mxq(x, axis, fmt="e4m3"):
    dtype, down = {"e4m3": (ml_dtypes.float8_e4m3fn, 7), "e5m2": (ml_dtypes.float8_e5m2, 14)}[fmt]
    v = np.moveaxis(np.asarray(x, np.float32).astype(ml_dtypes.bfloat16).astype(np.float64), axis, -1)
    blocks = v.reshape(v.shape[:-1] + (-1, 32))
    amax = np.abs(blocks).max(-1, keepdims=True)
    byte = np.maximum(np.where(amax > 0, np.frexp(amax)[1] - 1 + 127, 0) - down, 1)
    scale = np.exp2(byte - 127.0)
    codes = (blocks / scale).astype(np.float32).astype(dtype).astype(np.float64)
    return np.moveaxis((codes * scale).reshape(v.shape), -1, axis)


WIDE = False


def mx_kscale(k):
    if not WIDE:
        return np.ones(k)
    levels = np.array([10, -10, 5, -5, 0])
    if k % 512:
        return np.exp2(np.random.permutation(np.resize(levels, k // 32))).repeat(32)
    a = np.empty((k // 512, 16))
    for p in range(k // 512):
        a[p, :8] = np.random.permutation(np.resize(levels, 8))
        for g in range(8):
            far = levels[np.abs(levels - a[p, g]) >= 10]
            a[p, g + 8] = far[np.random.randint(len(far))]
    return np.exp2(a.ravel()).repeat(32)


BF16 = ml_dtypes.bfloat16


def bf(x):
    return np.asarray(x, np.float32).astype(BF16)


def f64(x):
    return np.asarray(x).astype(np.float64)


B, T, C, H, D, R = 4, 1024, 1024, 4, 128, 512
EPS = 1e-6
THETA = 10000.0


def rmsnorm(v, w):
    var = np.mean(v * v, axis=-1, keepdims=True)
    return v * (1.0 / np.sqrt(var + EPS)) * w


def rope(v, cos, sin):
    re, im = v[..., 0::2], v[..., 1::2]
    c, s = cos[None, :, None, :], sin[None, :, None, :]
    return np.stack([re * c - im * s, re * s + im * c], axis=-1).reshape(v.shape)


def setup_inputs():
    s, t = mx_kscale(C), mx_kscale(R)
    ang = np.outer(np.arange(T), 1.0 / THETA ** (np.arange(0, D, 2) / D))
    return {"x": bf(np.random.standard_normal((B, T, C)) * s),
            "w_kv_down": bf(np.random.standard_normal((R, C)) / np.sqrt(C) / s[None, :] * t[:, None]),
            "w_kv_up": bf(np.random.standard_normal((2 * H * D, R)) / np.sqrt(R) / t[None, :]),
            "k_norm_w": bf(1.0 + 0.1 * np.random.standard_normal(D)),
            "freqs_cos": bf(np.cos(ang)), "freqs_sin": bf(np.sin(ang))}


def reference(x, w_kv_down, w_kv_up, k_norm_w, freqs_cos, freqs_sin):
    latent = mxq(f64(x), 2, "e4m3") @ mxq(f64(w_kv_down), 1, "e4m3").T
    kv = (mxq(latent, 2, "e4m3") @ mxq(f64(w_kv_up), 1, "e4m3").T).reshape(B, T, 2, H, D)
    xk, xv = kv[:, :, 0], kv[:, :, 1]
    return rope(rmsnorm(xk, f64(k_norm_w)), f64(freqs_cos), f64(freqs_sin)), xv

@@ -1,0 +1,292 @@
+from contextlib import ExitStack
+
+import concourse.mybir as mybir
+from concourse.masks import make_identity
+
+F32 = mybir.dt.float32
+BF16 = mybir.dt.bfloat16
+U32 = mybir.dt.uint32
+U8 = mybir.dt.uint8
+FP8X4 = mybir.dt.float8_e4m3fn_x4
+ALU = mybir.AluOpType
+ACT = mybir.ActivationFunctionType
+
+P = 128
+PACK = 4
+K_PASS = P * PACK
+
+TOKENS = 4 * 1024
+SEQ = 1024
+C = 1024
+R = 512
+HEADS = 4
+D = 128
+HALF_D = D // 2
+KEY_COLS = HEADS * D
+EPS = 1e-6
+
+C_PASSES = C // K_PASS
+N_TILES = TOKENS // P
+SEQ_TILES = SEQ // P
+PAIR = 2
+N_PAIRS = N_TILES // PAIR
+UNIT_COLS = PAIR * 2 * P
+WEIGHT_UNITS = 2
+
+FLOPS = 2 * TOKENS * C * R + 2 * TOKENS * R * 2 * KEY_COLS
+
+
+def block(i):
+    return slice(i * P, (i + 1) * P)
+
+
+def channel_blocks(rows):
+    twins = rows.bitcast(F32).rearrange("o (g q u) -> o g u q", g=C_PASSES, u=2)
+    return [[twins[:, g, u, :] for u in range(2)] for g in range(C_PASSES)]
+
+
+def feature_blocks(rows_a, rows_b):
+    blocks = []
+    for rows in (rows_a, rows_b):
+        twins = rows.bitcast(F32).rearrange("o (q u) -> o u q", u=2)
+        blocks.append([twins[:, u, :] for u in range(2)])
+    return blocks
+
+
+def tile_mla_pa_t_kernel(
+    tc, x, w_kv_down, w_kv_up, k_norm_w, freqs_cos, freqs_sin, out_0, out_1
+):
+    nc = tc.nc
+    x_rows = x.flatten_outer_dims().rearrange("(s p n) c -> s p n c", p=P, n=PAIR)
+    k_rows = out_0.rearrange("b t h d -> (b t) (h d)").rearrange("(s p n) f -> s p n f", p=P, n=PAIR)
+    v_rows = out_1.rearrange("b t h d -> (b t) (h d)").rearrange("(s p n) f -> s p n f", p=P, n=PAIR)
+
+    with ExitStack() as stack:
+        stack.enter_context(tc.manual_schedule())
+        const = stack.enter_context(tc.tile_pool(name="const", bufs=1))
+        x_pool = stack.enter_context(tc.tile_pool(name="x", bufs=N_PAIRS))
+        work = stack.enter_context(tc.tile_pool(name="work", bufs=3))
+
+        wd_sb = const.tile([P, PACK, C], BF16)
+        wu_sb = const.tile([P, 2 * HEADS, R], BF16)
+        for i in range(WEIGHT_UNITS):
+            rows = slice(PAIR * i, PAIR * (i + 1))
+            nc.sync.dma_start(out=wd_sb[:, rows, :], in_=w_kv_down.rearrange("(p t) c -> p t c", t=PACK)[:, rows, :])
+        x_sb = []
+        for s in range(N_PAIRS):
+            x_pair = x_pool.tile([P, PAIR, C], BF16)
+            nc.sync.dma_start(out=x_pair[:], in_=x_rows[s])
+            x_sb.append(x_pair)
+        nc.sync.dma_start(out=wu_sb[:], in_=w_kv_up.rearrange("(b p) r -> p b r", p=P))
+
+        cos_sb = const.tile([P, SEQ_TILES, HALF_D], BF16)
+        sin_sb = const.tile([P, SEQ_TILES, HALF_D], BF16)
+        gain_sb = const.tile([P, HALF_D, 2], BF16)
+        nc.scalar.dma_start(
+            out=cos_sb[:].rearrange("p (s n) j -> p s n j", n=PAIR),
+            in_=freqs_cos.rearrange("(s p n) j -> p s n j", p=P, n=PAIR),
+        )
+        nc.scalar.dma_start(
+            out=sin_sb[:].rearrange("p (s n) j -> p s n j", n=PAIR),
+            in_=freqs_sin.rearrange("(s p n) j -> p s n j", p=P, n=PAIR),
+        )
+        nc.scalar.dma_start(out=gain_sb[:].rearrange("p j e -> p (j e)"), in_=k_norm_w.partition_broadcast(P))
+
+        identity = const.tile([P, P], F32)
+        make_identity(nc, identity[:])
+        eps = const.tile([P, 1], F32)
+        nc.vector.memset(eps[:], EPS)
+        table_warmer = const.tile([P, 1], F32)
+        nc.scalar.activation(out=table_warmer[:], in_=eps[:], func=ACT.Abs_reciprocal_sqrt)
+
+        signed_gain = const.tile([P, HALF_D, 2], F32)
+        nc.vector.tensor_copy(out=signed_gain[:, :, 0], in_=gain_sb[:, :, 0])
+        nc.vector.tensor_scalar_mul(out=signed_gain[:, :, 1], in0=gain_sb[:, :, 1], scalar1=-1.0)
+        rope_table = const.tile([P, SEQ_TILES, 2, HALF_D, 2], F32)
+        table_shape = [P, SEQ_TILES, HALF_D, 2]
+        nc.vector.tensor_tensor(
+            out=rope_table[:, :, 0],
+            in0=cos_sb[:].unsqueeze(3).to_broadcast(table_shape),
+            in1=gain_sb[:].unsqueeze(1).to_broadcast(table_shape),
+            op=ALU.mult,
+        )
+        nc.vector.tensor_tensor(
+            out=rope_table[:, :, 1],
+            in0=sin_sb[:].unsqueeze(3).to_broadcast(table_shape),
+            in1=signed_gain[:].unsqueeze(1).to_broadcast(table_shape),
+            op=ALU.mult,
+        )
+
+        wd_codes = const.tile([P, WEIGHT_UNITS * UNIT_COLS], U32, align_bytes=64)
+        wd_scales = const.tile([P, WEIGHT_UNITS * UNIT_COLS], U8, align_bytes=64)
+        wu_codes = const.tile([P, WEIGHT_UNITS * UNIT_COLS], U32, align_bytes=64)
+        wu_scales = const.tile([P, WEIGHT_UNITS * UNIT_COLS], U8, align_bytes=64)
+        latent_codes = const.tile([P, N_TILES * P], U32, align_bytes=64)
+        latent_scales = const.tile([P, N_TILES * P], U8, align_bytes=64)
+
+        FIRST_X = WEIGHT_UNITS
+        FIRST_UP = FIRST_X + N_PAIRS
+        N_UNITS = FIRST_UP + WEIGHT_UNITS
+
+        unit_blocks = []
+        unit_codes = {}
+        for i in range(WEIGHT_UNITS):
+            unit_blocks.append([channel_blocks(wd_sb[:, PAIR * i + n, :]) for n in range(PAIR)])
+        for s in range(N_PAIRS):
+            unit_blocks.append([channel_blocks(x_sb[s][:, n, :]) for n in range(PAIR)])
+        for i in range(WEIGHT_UNITS):
+            unit_blocks.append(
+                [feature_blocks(wu_sb[:, 4 * i + 2 * n, :], wu_sb[:, 4 * i + 2 * n + 1, :]) for n in range(PAIR)]
+            )
+        for i in range(WEIGHT_UNITS):
+            columns = slice(i * UNIT_COLS, (i + 1) * UNIT_COLS)
+            unit_codes[i] = (wd_codes[:, columns], wd_scales[:, columns])
+            unit_codes[FIRST_UP + i] = (wu_codes[:, columns], wu_scales[:, columns])
+
+        twin_banks, grouped, latent_banks, latent_grouped = {}, {}, {}, {}
+
+        with tc.psum_pool(name="phase1", bufs=4, reuse_waits="tile") as psum:
+
+            def transpose_unit(u):
+                twin_banks[u] = []
+                for n in range(PAIR):
+                    bank = psum.tile([P, 2, 2, P], F32, tag="twins")
+                    for a in range(2):
+                        for half in range(2):
+                            nc.tensor.transpose(bank[:, a, half, :], unit_blocks[u][n][a][half], identity[:])
+                    twin_banks[u].append(bank)
+
+            def group_unit(u):
+                grouped[u] = work.tile([P, UNIT_COLS * PACK], BF16, align_bytes=64, name="grouped")
+                words = grouped[u][:].bitcast(F32).rearrange("q (n a r u) -> q n a r u", n=PAIR, a=2, u=2)
+                nc.scalar.copy(out=words[:, 0], in_=twin_banks[u][0][:].rearrange("q a u r -> q a r u"))
+                nc.vector.tensor_copy(out=words[:, 1], in_=twin_banks[u][1][:].rearrange("q a u r -> q a r u"))
+
+            def quantise_unit(u):
+                if u not in unit_codes:
+                    x_codes = work.tile([P, UNIT_COLS], U32, align_bytes=64)
+                    x_scales = work.tile([P, UNIT_COLS], U8, align_bytes=64)
+                    unit_codes[u] = (x_codes[:], x_scales[:])
+                codes, scales = unit_codes[u]
+                nc.vector.quantize_mx(out=codes.bitcast(FP8X4), scales=scales, in_=grouped[u][:])
+
+            def latent_passes(s):
+                x_codes, x_scales = unit_codes[FIRST_X + s]
+                latent_banks[s] = []
+                for n in range(PAIR):
+                    bank = psum.tile([P, PACK, P], F32, tag="latent")
+                    for t in range(PACK):
+                        for g in range(C_PASSES):
+                            nc.tensor.matmul_mx(
+                                out=bank[:, t, :],
+                                lhsT=wd_codes[:, block(t * C_PASSES + g)].bitcast(FP8X4),
+                                lhsT_scale=wd_scales[:, block(t * C_PASSES + g)],
+                                rhs=x_codes[:, block(n * C_PASSES + g)].bitcast(FP8X4),
+                                rhs_scale=x_scales[:, block(n * C_PASSES + g)],
+                                start=(g == 0),
+                                stop=(g == C_PASSES - 1),
+                            )
+                    latent_banks[s].append(bank)
+
+            def group_latent(s):
+                latent_grouped[s] = work.tile([P, PAIR, P, PACK], BF16, align_bytes=64, name="latent_grouped")
+                for n in range(PAIR):
+                    nc.scalar.copy(out=latent_grouped[s][:, n], in_=latent_banks[s][n][:].rearrange("p t r -> p r t"))
+
+            def quantise_latent(s):
+                columns = slice(s * PAIR * P, (s + 1) * PAIR * P)
+                nc.vector.quantize_mx(
+                    out=latent_codes[:, columns].bitcast(FP8X4),
+                    scales=latent_scales[:, columns],
+                    in_=latent_grouped[s][:].rearrange("p n r t -> p (n r t)"),
+                )
+
+            for j in range(N_UNITS + 3):
+                if j < N_UNITS:
+                    transpose_unit(j)
+                if 0 <= j - 1 < N_UNITS:
+                    group_unit(j - 1)
+                if 0 <= j - 2 < N_UNITS:
+                    quantise_unit(j - 2)
+                s = j - 3 - FIRST_X
+                if 0 <= s < N_PAIRS:
+                    latent_passes(s)
+                if 0 <= s - 1 < N_PAIRS:
+                    group_latent(s - 1)
+                if 0 <= s - 2 < N_PAIRS:
+                    quantise_latent(s - 2)
+
+        k_banks, v_banks, sum_squares, rstd, products, k_out, v_out = {}, {}, {}, {}, {}, {}, {}
+
+        with tc.psum_pool(name="phase2", bufs=1, reuse_waits="tile") as psum:
+
+            def kv_passes(k):
+                k_banks[k] = psum.tile([P, HEADS, D], F32, tag="k", bufs=5, name="k_bank")
+                v_banks[k] = psum.tile([P, KEY_COLS], F32, tag="v", bufs=3, name="v_bank")
+                for bank, first_col in ((k_banks[k][:].rearrange("p h d -> p (h d)"), 0), (v_banks[k][:], KEY_COLS)):
+                    nc.tensor.matmul_mx(
+                        out=bank,
+                        lhsT=latent_codes[:, block(k)].bitcast(FP8X4),
+                        lhsT_scale=latent_scales[:, block(k)],
+                        rhs=wu_codes[:, first_col : first_col + KEY_COLS].bitcast(FP8X4),
+                        rhs_scale=wu_scales[:, first_col : first_col + KEY_COLS],
+                        start=True,
+                        stop=True,
+                    )
+
+            def sum_key_squares(k):
+                squares = work.tile([P, HEADS, D], F32)
+                sum_squares[k] = work.tile([P, HEADS], F32, name="sum_squares")
+                for h in range(HEADS):
+                    nc.scalar.activation(
+                        out=squares[:, h], in_=k_banks[k][:, h], func=ACT.Square, accum_out=sum_squares[k][:, h : h + 1]
+                    )
+
+            def copy_values(k):
+                if k % PAIR == 0:
+                    v_out[k // PAIR] = work.tile([P, PAIR, KEY_COLS], F32, name="v_out")
+                nc.scalar.copy(out=v_out[k // PAIR][:, k % PAIR, :], in_=v_banks[k][:])
+                if k % PAIR == PAIR - 1:
+                    nc.sync.dma_start(out=v_rows[k // PAIR], in_=v_out[k // PAIR][:])
+
+            def reciprocal_rms(k):
+                rstd[k] = work.tile([P, HEADS], F32, name="rstd")
+                nc.scalar.activation(
+                    out=rstd[k][:], in_=sum_squares[k][:], func=ACT.Abs_reciprocal_sqrt, scale=1.0 / D, bias=eps[:]
+                )
+
+            def multiply_keys(k):
+                products[k] = work.tile([P, HEADS, 2, HALF_D, 2], F32, name="products", bufs=4)
+                for h in range(HEADS):
+                    nc.vector.scalar_tensor_tensor(
+                        out=products[k][:, h].rearrange("p w j e -> p w (j e)"),
+                        in0=k_banks[k][:, h].unsqueeze(1).to_broadcast([P, 2, D]),
+                        scalar=rstd[k][:, h : h + 1],
+                        in1=rope_table[:, k % SEQ_TILES].rearrange("p w j e -> p w (j e)"),
+                        op0=ALU.mult,
+                        op1=ALU.mult,
+                    )
+
+            def sum_products(k):
+                if k % PAIR == 0:
+                    k_out[k // PAIR] = work.tile([P, PAIR, KEY_COLS], F32, name="k_out")
+                nc.gpsimd.tensor_tensor(
+                    out=k_out[k // PAIR][:, k % PAIR, :].rearrange("p (h j e) -> p h j e", h=HEADS, e=2),
+                    in0=products[k][:, :, 0],
+                    in1=products[k][:, :, 1, :, ::-1],
+                    op=ALU.add,
+                )
+                if k % PAIR == PAIR - 1:
+                    nc.sync.dma_start(out=k_rows[k // PAIR], in_=k_out[k // PAIR][:])
+
+            for j in range(N_TILES + 3):
+                if j < N_TILES:
+                    kv_passes(j)
+                if 0 <= j - 1 < N_TILES:
+                    sum_key_squares(j - 1)
+                    copy_values(j - 1)
+                    reciprocal_rms(j - 1)
+                if 0 <= j - 2 < N_TILES:
+                    multiply_keys(j - 2)
+                if 0 <= j - 3:
+                    sum_products(j - 3)

@@ -40,19 +40,6 @@ def block(i):
     return slice(i * P, (i + 1) * P)
 
 
-def channel_blocks(rows):
-    twins = rows.bitcast(F32).rearrange("o (g q u) -> o g u q", g=C_PASSES, u=2)
-    return [[twins[:, g, u, :] for u in range(2)] for g in range(C_PASSES)]
-
-
-def feature_blocks(rows_a, rows_b):
-    blocks = []
-    for rows in (rows_a, rows_b):
-        twins = rows.bitcast(F32).rearrange("o (q u) -> o u q", u=2)
-        blocks.append([twins[:, u, :] for u in range(2)])
-    return blocks
-
-
 def tile_mla_pa_t_kernel(
     tc, x, w_kv_down, w_kv_up, k_norm_w, freqs_cos, freqs_sin, out_0, out_1
 ):
@@ -69,28 +56,31 @@ def tile_mla_pa_t_kernel(
 
         wd_sb = const.tile([P, PACK, C], BF16)
         wu_sb = const.tile([P, 2 * HEADS, R], BF16)
-        for i in range(WEIGHT_UNITS):
+        cos_sb = const.tile([P, SEQ_TILES, HALF_D], BF16)
+        sin_sb = const.tile([P, SEQ_TILES, HALF_D], BF16)
+        gain_sb = const.tile([P, HALF_D, 2], BF16)
+
+        def load_wd(i):
             rows = slice(PAIR * i, PAIR * (i + 1))
             nc.sync.dma_start(out=wd_sb[:, rows, :], in_=w_kv_down.rearrange("(p t) c -> p t c", t=PACK)[:, rows, :])
+
+        def load_table(table, source):
+            nc.sync.dma_start(
+                out=table[:].rearrange("p (s n) j -> p s n j", n=PAIR),
+                in_=source.rearrange("(s p n) j -> p s n j", p=P, n=PAIR),
+            )
+
+        load_wd(0)
+        nc.sync.dma_start(out=gain_sb[:].rearrange("p j e -> p (j e)"), in_=k_norm_w.partition_broadcast(P))
+        load_table(cos_sb, freqs_cos)
+        load_wd(1)
+        load_table(sin_sb, freqs_sin)
         x_sb = []
         for s in range(N_PAIRS):
             x_pair = x_pool.tile([P, PAIR, C], BF16)
             nc.sync.dma_start(out=x_pair[:], in_=x_rows[s])
             x_sb.append(x_pair)
         nc.sync.dma_start(out=wu_sb[:], in_=w_kv_up.rearrange("(b p) r -> p b r", p=P))
-
-        cos_sb = const.tile([P, SEQ_TILES, HALF_D], BF16)
-        sin_sb = const.tile([P, SEQ_TILES, HALF_D], BF16)
-        gain_sb = const.tile([P, HALF_D, 2], BF16)
-        nc.scalar.dma_start(
-            out=cos_sb[:].rearrange("p (s n) j -> p s n j", n=PAIR),
-            in_=freqs_cos.rearrange("(s p n) j -> p s n j", p=P, n=PAIR),
-        )
-        nc.scalar.dma_start(
-            out=sin_sb[:].rearrange("p (s n) j -> p s n j", n=PAIR),
-            in_=freqs_sin.rearrange("(s p n) j -> p s n j", p=P, n=PAIR),
-        )
-        nc.scalar.dma_start(out=gain_sb[:].rearrange("p j e -> p (j e)"), in_=k_norm_w.partition_broadcast(P))
 
         identity = const.tile([P, P], F32)
         make_identity(nc, identity[:])
@@ -128,39 +118,46 @@ def tile_mla_pa_t_kernel(
         FIRST_UP = FIRST_X + N_PAIRS
         N_UNITS = FIRST_UP + WEIGHT_UNITS
 
-        unit_blocks = []
+        unit_rows = []
         unit_codes = {}
         for i in range(WEIGHT_UNITS):
-            unit_blocks.append([channel_blocks(wd_sb[:, PAIR * i + n, :]) for n in range(PAIR)])
+            unit_rows.append(wd_sb[:, PAIR * i : PAIR * (i + 1), :].rearrange("p n c -> p (n c)"))
         for s in range(N_PAIRS):
-            unit_blocks.append([channel_blocks(x_sb[s][:, n, :]) for n in range(PAIR)])
+            unit_rows.append(x_sb[s][:].rearrange("p n c -> p (n c)"))
         for i in range(WEIGHT_UNITS):
-            unit_blocks.append(
-                [feature_blocks(wu_sb[:, 4 * i + 2 * n, :], wu_sb[:, 4 * i + 2 * n + 1, :]) for n in range(PAIR)]
-            )
+            unit_rows.append(wu_sb[:, 4 * i : 4 * i + 4, :].rearrange("p b r -> p (b r)"))
         for i in range(WEIGHT_UNITS):
             columns = slice(i * UNIT_COLS, (i + 1) * UNIT_COLS)
             unit_codes[i] = (wd_codes[:, columns], wd_scales[:, columns])
             unit_codes[FIRST_UP + i] = (wu_codes[:, columns], wu_scales[:, columns])
 
-        twin_banks, grouped, latent_banks, latent_grouped = {}, {}, {}, {}
+        sorted_twins, twin_banks, grouped, latent_banks, latent_grouped = {}, {}, {}, {}, {}
 
         with tc.psum_pool(name="phase1", bufs=4, reuse_waits="tile") as psum:
 
+            def twins_in_order(u):
+                return unit_rows[u].bitcast(F32).rearrange("p (g q u) -> p g u q", q=P, u=2)
+
+            def sort_unit(u):
+                sorted_twins[u] = work.tile([P, 2 * PAIR, 2, P], F32, name="sorted_twins")
+                nc.vector.tensor_copy(out=sorted_twins[u][:], in_=twins_in_order(u))
+
             def transpose_unit(u):
+                twins = twins_in_order(u) if u < FIRST_X else sorted_twins[u]
                 twin_banks[u] = []
                 for n in range(PAIR):
                     bank = psum.tile([P, 2, 2, P], F32, tag="twins")
                     for a in range(2):
                         for half in range(2):
-                            nc.tensor.transpose(bank[:, a, half, :], unit_blocks[u][n][a][half], identity[:])
+                            nc.tensor.transpose(bank[:, a, half, :], twins[:, 2 * n + a, half, :], identity[:])
                     twin_banks[u].append(bank)
 
             def group_unit(u):
                 grouped[u] = work.tile([P, UNIT_COLS * PACK], BF16, align_bytes=64, name="grouped")
                 words = grouped[u][:].bitcast(F32).rearrange("q (n a r u) -> q n a r u", n=PAIR, a=2, u=2)
                 nc.scalar.copy(out=words[:, 0], in_=twin_banks[u][0][:].rearrange("q a u r -> q a r u"))
-                nc.vector.tensor_copy(out=words[:, 1], in_=twin_banks[u][1][:].rearrange("q a u r -> q a r u"))
+                copy = nc.scalar.copy if u % 2 or u < FIRST_X else nc.vector.tensor_copy
+                copy(out=words[:, 1], in_=twin_banks[u][1][:].rearrange("q a u r -> q a r u"))
 
             def quantise_unit(u):
                 if u not in unit_codes:
@@ -204,6 +201,8 @@ def tile_mla_pa_t_kernel(
             for j in range(N_UNITS + 3):
                 if j < N_UNITS:
                     transpose_unit(j)
+                if FIRST_X <= j + 1 < N_UNITS:
+                    sort_unit(j + 1)
                 if 0 <= j - 1 < N_UNITS:
                     group_unit(j - 1)
                 if 0 <= j - 2 < N_UNITS:

@@ -32,6 +32,7 @@ PAIR = 2
 N_PAIRS = N_TILES // PAIR
 UNIT_COLS = PAIR * 2 * P
 WEIGHT_UNITS = 2
+PAIRS_BEFORE_UP = 8
 
 FLOPS = 2 * TOKENS * C * R + 2 * TOKENS * R * 2 * KEY_COLS
 
@@ -77,10 +78,11 @@ def tile_mla_pa_t_kernel(
         load_table(sin_sb, freqs_sin)
         x_sb = []
         for s in range(N_PAIRS):
+            if s == PAIRS_BEFORE_UP:
+                nc.sync.dma_start(out=wu_sb[:], in_=w_kv_up.rearrange("(b p) r -> p b r", p=P))
             x_pair = x_pool.tile([P, PAIR, C], BF16)
             nc.sync.dma_start(out=x_pair[:], in_=x_rows[s])
             x_sb.append(x_pair)
-        nc.sync.dma_start(out=wu_sb[:], in_=w_kv_up.rearrange("(b p) r -> p b r", p=P))
 
         identity = const.tile([P, P], F32)
         make_identity(nc, identity[:])
@@ -114,178 +116,204 @@ def tile_mla_pa_t_kernel(
         latent_codes = const.tile([P, N_TILES * P], U32, align_bytes=64)
         latent_scales = const.tile([P, N_TILES * P], U8, align_bytes=64)
 
-        FIRST_X = WEIGHT_UNITS
-        FIRST_UP = FIRST_X + N_PAIRS
-        N_UNITS = FIRST_UP + WEIGHT_UNITS
-
         unit_rows = []
         unit_codes = {}
-        for i in range(WEIGHT_UNITS):
-            unit_rows.append(wd_sb[:, PAIR * i : PAIR * (i + 1), :].rearrange("p n c -> p (n c)"))
+        pair_of_unit = {}
+
+        def add_weight_units(rows, codes, scales):
+            for i in range(WEIGHT_UNITS):
+                columns = slice(i * UNIT_COLS, (i + 1) * UNIT_COLS)
+                unit_codes[len(unit_rows)] = (codes[:, columns], scales[:, columns])
+                unit_rows.append(rows[:, i * UNIT_COLS * PACK : (i + 1) * UNIT_COLS * PACK])
+
+        add_weight_units(wd_sb[:].rearrange("p t c -> p (t c)"), wd_codes, wd_scales)
         for s in range(N_PAIRS):
+            if s == PAIRS_BEFORE_UP:
+                add_weight_units(wu_sb[:].rearrange("p b r -> p (b r)"), wu_codes, wu_scales)
+            pair_of_unit[len(unit_rows)] = s
             unit_rows.append(x_sb[s][:].rearrange("p n c -> p (n c)"))
-        for i in range(WEIGHT_UNITS):
-            unit_rows.append(wu_sb[:, 4 * i : 4 * i + 4, :].rearrange("p b r -> p (b r)"))
-        for i in range(WEIGHT_UNITS):
-            columns = slice(i * UNIT_COLS, (i + 1) * UNIT_COLS)
-            unit_codes[i] = (wd_codes[:, columns], wd_scales[:, columns])
-            unit_codes[FIRST_UP + i] = (wu_codes[:, columns], wu_scales[:, columns])
+        N_UNITS = len(unit_rows)
+        AS_THEY_LIE = WEIGHT_UNITS + 1
 
         sorted_twins, twin_banks, grouped, latent_banks, latent_grouped = {}, {}, {}, {}, {}
-
-        with tc.psum_pool(name="phase1", bufs=4, reuse_waits="tile") as psum:
-
-            def twins_in_order(u):
-                return unit_rows[u].bitcast(F32).rearrange("p (g q u) -> p g u q", q=P, u=2)
-
-            def sort_unit(u):
-                sorted_twins[u] = work.tile([P, 2 * PAIR, 2, P], F32, name="sorted_twins")
-                nc.vector.tensor_copy(out=sorted_twins[u][:], in_=twins_in_order(u))
-
-            def transpose_unit(u):
-                twins = twins_in_order(u) if u < FIRST_X else sorted_twins[u]
-                twin_banks[u] = []
-                for n in range(PAIR):
-                    bank = psum.tile([P, 2, 2, P], F32, tag="twins")
-                    for a in range(2):
-                        for half in range(2):
-                            nc.tensor.transpose(bank[:, a, half, :], twins[:, 2 * n + a, half, :], identity[:])
-                    twin_banks[u].append(bank)
-
-            def group_unit(u):
-                grouped[u] = work.tile([P, UNIT_COLS * PACK], BF16, align_bytes=64, name="grouped")
-                words = grouped[u][:].bitcast(F32).rearrange("q (n a r u) -> q n a r u", n=PAIR, a=2, u=2)
-                nc.scalar.copy(out=words[:, 0], in_=twin_banks[u][0][:].rearrange("q a u r -> q a r u"))
-                copy = nc.scalar.copy if u % 2 or u < FIRST_X else nc.vector.tensor_copy
-                copy(out=words[:, 1], in_=twin_banks[u][1][:].rearrange("q a u r -> q a r u"))
-
-            def quantise_unit(u):
-                if u not in unit_codes:
-                    x_codes = work.tile([P, UNIT_COLS], U32, align_bytes=64)
-                    x_scales = work.tile([P, UNIT_COLS], U8, align_bytes=64)
-                    unit_codes[u] = (x_codes[:], x_scales[:])
-                codes, scales = unit_codes[u]
-                nc.vector.quantize_mx(out=codes.bitcast(FP8X4), scales=scales, in_=grouped[u][:])
-
-            def latent_passes(s):
-                x_codes, x_scales = unit_codes[FIRST_X + s]
-                latent_banks[s] = []
-                for n in range(PAIR):
-                    bank = psum.tile([P, PACK, P], F32, tag="latent")
-                    for t in range(PACK):
-                        for g in range(C_PASSES):
-                            nc.tensor.matmul_mx(
-                                out=bank[:, t, :],
-                                lhsT=wd_codes[:, block(t * C_PASSES + g)].bitcast(FP8X4),
-                                lhsT_scale=wd_scales[:, block(t * C_PASSES + g)],
-                                rhs=x_codes[:, block(n * C_PASSES + g)].bitcast(FP8X4),
-                                rhs_scale=x_scales[:, block(n * C_PASSES + g)],
-                                start=(g == 0),
-                                stop=(g == C_PASSES - 1),
-                            )
-                    latent_banks[s].append(bank)
-
-            def group_latent(s):
-                latent_grouped[s] = work.tile([P, PAIR, P, PACK], BF16, align_bytes=64, name="latent_grouped")
-                for n in range(PAIR):
-                    nc.scalar.copy(out=latent_grouped[s][:, n], in_=latent_banks[s][n][:].rearrange("p t r -> p r t"))
-
-            def quantise_latent(s):
-                columns = slice(s * PAIR * P, (s + 1) * PAIR * P)
-                nc.vector.quantize_mx(
-                    out=latent_codes[:, columns].bitcast(FP8X4),
-                    scales=latent_scales[:, columns],
-                    in_=latent_grouped[s][:].rearrange("p n r t -> p (n r t)"),
-                )
-
-            for j in range(N_UNITS + 3):
-                if j < N_UNITS:
-                    transpose_unit(j)
-                if FIRST_X <= j + 1 < N_UNITS:
-                    sort_unit(j + 1)
-                if 0 <= j - 1 < N_UNITS:
-                    group_unit(j - 1)
-                if 0 <= j - 2 < N_UNITS:
-                    quantise_unit(j - 2)
-                s = j - 3 - FIRST_X
-                if 0 <= s < N_PAIRS:
-                    latent_passes(s)
-                if 0 <= s - 1 < N_PAIRS:
-                    group_latent(s - 1)
-                if 0 <= s - 2 < N_PAIRS:
-                    quantise_latent(s - 2)
-
         k_banks, v_banks, sum_squares, rstd, products, k_out, v_out = {}, {}, {}, {}, {}, {}, {}
 
-        with tc.psum_pool(name="phase2", bufs=1, reuse_waits="tile") as psum:
+        psum = stack.enter_context(tc.psum_pool(name="banks", bufs=4, reuse_waits="tile"))
 
-            def kv_passes(k):
-                k_banks[k] = psum.tile([P, HEADS, D], F32, tag="k", bufs=5, name="k_bank")
-                v_banks[k] = psum.tile([P, KEY_COLS], F32, tag="v", bufs=3, name="v_bank")
-                for bank, first_col in ((k_banks[k][:].rearrange("p h d -> p (h d)"), 0), (v_banks[k][:], KEY_COLS)):
-                    nc.tensor.matmul_mx(
-                        out=bank,
-                        lhsT=latent_codes[:, block(k)].bitcast(FP8X4),
-                        lhsT_scale=latent_scales[:, block(k)],
-                        rhs=wu_codes[:, first_col : first_col + KEY_COLS].bitcast(FP8X4),
-                        rhs_scale=wu_scales[:, first_col : first_col + KEY_COLS],
-                        start=True,
-                        stop=True,
-                    )
+        def sort_unit(u):
+            sorted_twins[u] = work.tile([P, 2, 2 * PAIR, P], F32, name="sorted_twins")
+            nc.vector.tensor_copy(
+                out=sorted_twins[u][:].rearrange("p u g (r i) -> p (g r) u i", i=4),
+                in_=unit_rows[u].bitcast(F32).rearrange("p (r i u) -> p r u i", i=4, u=2),
+            )
 
-            def sum_key_squares(k):
-                squares = work.tile([P, HEADS, D], F32)
-                sum_squares[k] = work.tile([P, HEADS], F32, name="sum_squares")
-                for h in range(HEADS):
-                    nc.scalar.activation(
-                        out=squares[:, h], in_=k_banks[k][:, h], func=ACT.Square, accum_out=sum_squares[k][:, h : h + 1]
-                    )
+        def transpose_unit(u):
+            if u < AS_THEY_LIE:
+                twins = unit_rows[u].bitcast(F32).rearrange("p (g q u) -> p u g q", q=P, u=2)
+            else:
+                twins = sorted_twins[u]
+            twin_banks[u] = []
+            for n in range(PAIR):
+                bank = psum.tile([P, 2, 2, P], F32, tag="twins", name="twin_bank")
+                for a in range(2):
+                    for half in range(2):
+                        nc.tensor.transpose(bank[:, a, half, :], twins[:, half, 2 * n + a, :], identity[:])
+                twin_banks[u].append(bank)
 
-            def copy_values(k):
-                if k % PAIR == 0:
-                    v_out[k // PAIR] = work.tile([P, PAIR, KEY_COLS], F32, name="v_out")
-                nc.scalar.copy(out=v_out[k // PAIR][:, k % PAIR, :], in_=v_banks[k][:])
-                if k % PAIR == PAIR - 1:
-                    nc.sync.dma_start(out=v_rows[k // PAIR], in_=v_out[k // PAIR][:])
+        def group_unit(u):
+            grouped[u] = work.tile([P, UNIT_COLS * PACK], BF16, align_bytes=64, name="grouped")
+            words = grouped[u][:].bitcast(F32).rearrange("q (n a r u) -> q n a r u", n=PAIR, a=2, u=2)
+            nc.scalar.copy(out=words[:, 0], in_=twin_banks[u][0][:].rearrange("q a u r -> q a r u"))
+            copy = nc.scalar.copy if u % 2 or u < WEIGHT_UNITS else nc.vector.tensor_copy
+            copy(out=words[:, 1], in_=twin_banks[u][1][:].rearrange("q a u r -> q a r u"))
 
-            def reciprocal_rms(k):
-                rstd[k] = work.tile([P, HEADS], F32, name="rstd")
+        def quantise_unit(u):
+            if u not in unit_codes:
+                x_codes = work.tile([P, UNIT_COLS], U32, align_bytes=64)
+                x_scales = work.tile([P, UNIT_COLS], U8, align_bytes=64)
+                unit_codes[u] = (x_codes[:], x_scales[:])
+            codes, scales = unit_codes[u]
+            nc.vector.quantize_mx(out=codes.bitcast(FP8X4), scales=scales, in_=grouped[u][:])
+
+        def latent_passes(u):
+            x_codes, x_scales = unit_codes[u]
+            latent_banks[u] = []
+            for n in range(PAIR):
+                bank = psum.tile([P, PACK, P], F32, tag="latent", name="latent_bank")
+                for t in range(PACK):
+                    for g in range(C_PASSES):
+                        nc.tensor.matmul_mx(
+                            out=bank[:, t, :],
+                            lhsT=wd_codes[:, block(t * C_PASSES + g)].bitcast(FP8X4),
+                            lhsT_scale=wd_scales[:, block(t * C_PASSES + g)],
+                            rhs=x_codes[:, block(n * C_PASSES + g)].bitcast(FP8X4),
+                            rhs_scale=x_scales[:, block(n * C_PASSES + g)],
+                            start=(g == 0),
+                            stop=(g == C_PASSES - 1),
+                        )
+                latent_banks[u].append(bank)
+
+        def group_latent(u):
+            latent_grouped[u] = work.tile([P, PAIR, P, PACK], BF16, align_bytes=64, name="latent_grouped")
+            for n in range(PAIR):
+                nc.scalar.copy(out=latent_grouped[u][:, n], in_=latent_banks[u][n][:].rearrange("p t r -> p r t"))
+
+        def quantise_latent(u):
+            s = pair_of_unit[u]
+            columns = slice(s * PAIR * P, (s + 1) * PAIR * P)
+            nc.vector.quantize_mx(
+                out=latent_codes[:, columns].bitcast(FP8X4),
+                scales=latent_scales[:, columns],
+                in_=latent_grouped[u][:].rearrange("p n r t -> p (n r t)"),
+            )
+
+        def kv_passes(k):
+            k_banks[k] = psum.tile([P, HEADS, D], F32, tag="twins", name="k_bank")
+            v_banks[k] = psum.tile([P, KEY_COLS], F32, tag="latent", name="v_bank")
+            for bank, first_col in ((k_banks[k][:].rearrange("p h d -> p (h d)"), 0), (v_banks[k][:], KEY_COLS)):
+                nc.tensor.matmul_mx(
+                    out=bank,
+                    lhsT=latent_codes[:, block(k)].bitcast(FP8X4),
+                    lhsT_scale=latent_scales[:, block(k)],
+                    rhs=wu_codes[:, first_col : first_col + KEY_COLS].bitcast(FP8X4),
+                    rhs_scale=wu_scales[:, first_col : first_col + KEY_COLS],
+                    start=True,
+                    stop=True,
+                )
+
+        def sum_key_squares(k):
+            squares = work.tile([P, HEADS, D], F32)
+            sum_squares[k] = work.tile([P, HEADS], F32, name="sum_squares")
+            for h in range(HEADS):
                 nc.scalar.activation(
-                    out=rstd[k][:], in_=sum_squares[k][:], func=ACT.Abs_reciprocal_sqrt, scale=1.0 / D, bias=eps[:]
+                    out=squares[:, h], in_=k_banks[k][:, h], func=ACT.Square, accum_out=sum_squares[k][:, h : h + 1]
                 )
 
-            def multiply_keys(k):
-                products[k] = work.tile([P, HEADS, 2, HALF_D, 2], F32, name="products", bufs=4)
-                for h in range(HEADS):
-                    nc.vector.scalar_tensor_tensor(
-                        out=products[k][:, h].rearrange("p w j e -> p w (j e)"),
-                        in0=k_banks[k][:, h].unsqueeze(1).to_broadcast([P, 2, D]),
-                        scalar=rstd[k][:, h : h + 1],
-                        in1=rope_table[:, k % SEQ_TILES].rearrange("p w j e -> p w (j e)"),
-                        op0=ALU.mult,
-                        op1=ALU.mult,
-                    )
+        def copy_values(k):
+            if k % PAIR == 0:
+                v_out[k // PAIR] = work.tile([P, PAIR, KEY_COLS], F32, name="v_out")
+            copy = nc.vector.tensor_copy if k % 4 == 3 else nc.scalar.copy
+            copy(out=v_out[k // PAIR][:, k % PAIR, :], in_=v_banks[k][:])
+            if k % PAIR == PAIR - 1:
+                nc.sync.dma_start(out=v_rows[k // PAIR], in_=v_out[k // PAIR][:])
 
-            def sum_products(k):
-                if k % PAIR == 0:
-                    k_out[k // PAIR] = work.tile([P, PAIR, KEY_COLS], F32, name="k_out")
-                nc.gpsimd.tensor_tensor(
-                    out=k_out[k // PAIR][:, k % PAIR, :].rearrange("p (h j e) -> p h j e", h=HEADS, e=2),
-                    in0=products[k][:, :, 0],
-                    in1=products[k][:, :, 1, :, ::-1],
-                    op=ALU.add,
+        def reciprocal_rms(k):
+            rstd[k] = work.tile([P, HEADS], F32, name="rstd")
+            nc.scalar.activation(
+                out=rstd[k][:], in_=sum_squares[k][:], func=ACT.Abs_reciprocal_sqrt, scale=1.0 / D, bias=eps[:]
+            )
+
+        def multiply_keys(k):
+            if k % PAIR == 0:
+                products[k // PAIR] = work.tile([P, PAIR, HEADS, 2, HALF_D, 2], F32, name="products")
+            for h in range(HEADS):
+                nc.vector.scalar_tensor_tensor(
+                    out=products[k // PAIR][:, k % PAIR, h].rearrange("p w j e -> p w (j e)"),
+                    in0=k_banks[k][:, h].unsqueeze(1).to_broadcast([P, 2, D]),
+                    scalar=rstd[k][:, h : h + 1],
+                    in1=rope_table[:, k % SEQ_TILES].rearrange("p w j e -> p w (j e)"),
+                    op0=ALU.mult,
+                    op1=ALU.mult,
                 )
+
+        def sum_products(s, tiles, engine):
+            if tiles.start == 0:
+                k_out[s] = work.tile([P, PAIR, HEADS, HALF_D, 2], F32, name="k_out")
+            engine.tensor_tensor(
+                out=k_out[s][:, tiles].rearrange("p n h j e -> p (n h) j e"),
+                in0=products[s][:, tiles, :, 0].rearrange("p n h j e -> p (n h) j e"),
+                in1=products[s][:, tiles, :, 1].rearrange("p n h j e -> p (n h) j e")[:, :, :, ::-1],
+                op=ALU.add,
+            )
+            nc.sync.dma_start(
+                out=k_rows[s][:, tiles], in_=k_out[s][:, tiles].rearrange("p n h j e -> p n (h j e)")
+            )
+
+        for j in range(N_UNITS + 1):
+            if j < N_UNITS:
+                transpose_unit(j)
+            if AS_THEY_LIE <= j + 1 < N_UNITS:
+                sort_unit(j + 1)
+            if 0 <= j - 1:
+                group_unit(j - 1)
+            if 0 <= j - 2:
+                quantise_unit(j - 2)
+            if j - 3 in pair_of_unit:
+                latent_passes(j - 3)
+            if j - 4 in pair_of_unit:
+                group_latent(j - 4)
+            if j - 5 in pair_of_unit:
+                quantise_latent(j - 5)
+
+        last = N_UNITS - 1
+        quantise_unit(last)
+        latent_passes(last - 1)
+        group_latent(last - 2)
+        quantise_latent(last - 3)
+        kv_passes(0)
+        kv_passes(1)
+        group_latent(last - 1)
+        quantise_latent(last - 2)
+        latent_passes(last)
+        sum_key_squares(0)
+        copy_values(0)
+        reciprocal_rms(0)
+        quantise_latent(last - 1)
+        multiply_keys(0)
+        group_latent(last)
+        quantise_latent(last)
+
+        for k in range(1, N_TILES):
+            if k > 1:
+                kv_passes(k)
+            sum_key_squares(k)
+            copy_values(k)
+            reciprocal_rms(k)
+            multiply_keys(k)
+            s = k // PAIR
+            if s < N_PAIRS - 1:
                 if k % PAIR == PAIR - 1:
-                    nc.sync.dma_start(out=k_rows[k // PAIR], in_=k_out[k // PAIR][:])
-
-            for j in range(N_TILES + 3):
-                if j < N_TILES:
-                    kv_passes(j)
-                if 0 <= j - 1 < N_TILES:
-                    sum_key_squares(j - 1)
-                    copy_values(j - 1)
-                    reciprocal_rms(j - 1)
-                if 0 <= j - 2 < N_TILES:
-                    multiply_keys(j - 2)
-                if 0 <= j - 3:
-                    sum_products(j - 3)
+                    sum_products(s, slice(0, PAIR), nc.gpsimd)
+            else:
+                n = k % PAIR
+                sum_products(s, slice(n, n + 1), nc.gpsimd if n == 0 else nc.vector)

@@ -31,7 +31,8 @@ SEQ_TILES = SEQ // P
 PAIR = 2
 N_PAIRS = N_TILES // PAIR
 UNIT_COLS = PAIR * 2 * P
-WEIGHT_UNITS = 2
+BANK_VALUES = 2 * P * PACK
+UP_UNITS = 2
 PAIRS_BEFORE_UP = 8
 
 FLOPS = 2 * TOKENS * C * R + 2 * TOKENS * R * 2 * KEY_COLS
@@ -61,21 +62,21 @@ def tile_mla_pa_t_kernel(
         sin_sb = const.tile([P, SEQ_TILES, HALF_D], BF16)
         gain_sb = const.tile([P, HALF_D, 2], BF16)
 
-        def load_wd(i):
-            rows = slice(PAIR * i, PAIR * (i + 1))
-            nc.sync.dma_start(out=wd_sb[:, rows, :], in_=w_kv_down.rearrange("(p t) c -> p t c", t=PACK)[:, rows, :])
-
         def load_table(table, source):
             nc.sync.dma_start(
                 out=table[:].rearrange("p (s n) j -> p s n j", n=PAIR),
                 in_=source.rearrange("(s p n) j -> p s n j", p=P, n=PAIR),
             )
 
-        load_wd(0)
+        def load_wd(t):
+            nc.sync.dma_start(out=wd_sb[:, t, :], in_=w_kv_down.rearrange("(p t) c -> p t c", t=PACK)[:, t, :])
+
         nc.sync.dma_start(out=gain_sb[:].rearrange("p j e -> p (j e)"), in_=k_norm_w.partition_broadcast(P))
         load_table(cos_sb, freqs_cos)
-        load_wd(1)
+        load_wd(0)
         load_table(sin_sb, freqs_sin)
+        for t in range(1, PACK):
+            load_wd(t)
         x_sb = []
         for s in range(N_PAIRS):
             if s == PAIRS_BEFORE_UP:
@@ -92,48 +93,37 @@ def tile_mla_pa_t_kernel(
         nc.scalar.activation(out=table_warmer[:], in_=eps[:], func=ACT.Abs_reciprocal_sqrt)
 
         signed_gain = const.tile([P, HALF_D, 2], F32)
+        rope_table = const.tile([P, SEQ_TILES, 2, HALF_D, 2], F32)
+
         nc.vector.tensor_copy(out=signed_gain[:, :, 0], in_=gain_sb[:, :, 0])
         nc.vector.tensor_scalar_mul(out=signed_gain[:, :, 1], in0=gain_sb[:, :, 1], scalar1=-1.0)
-        rope_table = const.tile([P, SEQ_TILES, 2, HALF_D, 2], F32)
-        table_shape = [P, SEQ_TILES, HALF_D, 2]
-        nc.vector.tensor_tensor(
-            out=rope_table[:, :, 0],
-            in0=cos_sb[:].unsqueeze(3).to_broadcast(table_shape),
-            in1=gain_sb[:].unsqueeze(1).to_broadcast(table_shape),
-            op=ALU.mult,
-        )
-        nc.vector.tensor_tensor(
-            out=rope_table[:, :, 1],
-            in0=sin_sb[:].unsqueeze(3).to_broadcast(table_shape),
-            in1=signed_gain[:].unsqueeze(1).to_broadcast(table_shape),
-            op=ALU.mult,
-        )
+        for row, angles, gain in ((0, cos_sb, gain_sb), (1, sin_sb, signed_gain)):
+            nc.vector.tensor_tensor(
+                out=rope_table[:, :, row],
+                in0=angles[:].unsqueeze(3).to_broadcast([P, SEQ_TILES, HALF_D, 2]),
+                in1=gain[:].unsqueeze(1).to_broadcast([P, SEQ_TILES, HALF_D, 2]),
+                op=ALU.mult,
+            )
 
-        wd_codes = const.tile([P, WEIGHT_UNITS * UNIT_COLS], U32, align_bytes=64)
-        wd_scales = const.tile([P, WEIGHT_UNITS * UNIT_COLS], U8, align_bytes=64)
-        wu_codes = const.tile([P, WEIGHT_UNITS * UNIT_COLS], U32, align_bytes=64)
-        wu_scales = const.tile([P, WEIGHT_UNITS * UNIT_COLS], U8, align_bytes=64)
+        wd_codes = const.tile([P, UP_UNITS * UNIT_COLS], U32, align_bytes=64)
+        wd_scales = const.tile([P, UP_UNITS * UNIT_COLS], U8, align_bytes=64)
+        wu_codes = const.tile([P, UP_UNITS * UNIT_COLS], U32, align_bytes=64)
+        wu_scales = const.tile([P, UP_UNITS * UNIT_COLS], U8, align_bytes=64)
         latent_codes = const.tile([P, N_TILES * P], U32, align_bytes=64)
         latent_scales = const.tile([P, N_TILES * P], U8, align_bytes=64)
 
         unit_rows = []
         unit_codes = {}
         pair_of_unit = {}
-
-        def add_weight_units(rows, codes, scales):
-            for i in range(WEIGHT_UNITS):
-                columns = slice(i * UNIT_COLS, (i + 1) * UNIT_COLS)
-                unit_codes[len(unit_rows)] = (codes[:, columns], scales[:, columns])
-                unit_rows.append(rows[:, i * UNIT_COLS * PACK : (i + 1) * UNIT_COLS * PACK])
-
-        add_weight_units(wd_sb[:].rearrange("p t c -> p (t c)"), wd_codes, wd_scales)
         for s in range(N_PAIRS):
             if s == PAIRS_BEFORE_UP:
-                add_weight_units(wu_sb[:].rearrange("p b r -> p (b r)"), wu_codes, wu_scales)
+                for i in range(UP_UNITS):
+                    columns = slice(i * UNIT_COLS, (i + 1) * UNIT_COLS)
+                    unit_codes[len(unit_rows)] = (wu_codes[:, columns], wu_scales[:, columns])
+                    unit_rows.append(wu_sb[:, 4 * i : 4 * (i + 1), :].rearrange("p b r -> p (b r)"))
             pair_of_unit[len(unit_rows)] = s
             unit_rows.append(x_sb[s][:].rearrange("p n c -> p (n c)"))
         N_UNITS = len(unit_rows)
-        AS_THEY_LIE = WEIGHT_UNITS + 1
 
         sorted_twins, twin_banks, grouped, latent_banks, latent_grouped = {}, {}, {}, {}, {}
         k_banks, v_banks, sum_squares, rstd, products, k_out, v_out = {}, {}, {}, {}, {}, {}, {}
@@ -141,31 +131,34 @@ def tile_mla_pa_t_kernel(
         psum = stack.enter_context(tc.psum_pool(name="banks", bufs=4, reuse_waits="tile"))
 
         def sort_unit(u):
-            sorted_twins[u] = work.tile([P, 2, 2 * PAIR, P], F32, name="sorted_twins")
-            nc.vector.tensor_copy(
-                out=sorted_twins[u][:].rearrange("p u g (r i) -> p (g r) u i", i=4),
-                in_=unit_rows[u].bitcast(F32).rearrange("p (r i u) -> p r u i", i=4, u=2),
+            twins = work.tile([P, 2 * PAIR, 2, P], F32, name="sorted_twins")
+            nc.vector.tensor_copy(out=twins[:], in_=twins_as_they_lie(unit_rows[u]))
+            sorted_twins[u] = twins[:]
+
+        def transpose_bank(groups):
+            bank = psum.tile([P, 2, 2, P], F32, tag="twins", name="twin_bank")
+            for a in range(2):
+                for half in range(2):
+                    nc.tensor.transpose(bank[:, a, half, :], groups[:, a, half, :], identity[:])
+            return bank
+
+        def group_bank(bank, values, copy):
+            copy(
+                out=values.bitcast(F32).rearrange("q (a r u) -> q a r u", a=2, u=2),
+                in_=bank[:].rearrange("q a u r -> q a r u"),
             )
 
+        def twins_as_they_lie(rows):
+            return rows.bitcast(F32).rearrange("p (g q u) -> p g u q", q=P, u=2)
+
         def transpose_unit(u):
-            if u < AS_THEY_LIE:
-                twins = unit_rows[u].bitcast(F32).rearrange("p (g q u) -> p u g q", q=P, u=2)
-            else:
-                twins = sorted_twins[u]
-            twin_banks[u] = []
-            for n in range(PAIR):
-                bank = psum.tile([P, 2, 2, P], F32, tag="twins", name="twin_bank")
-                for a in range(2):
-                    for half in range(2):
-                        nc.tensor.transpose(bank[:, a, half, :], twins[:, half, 2 * n + a, :], identity[:])
-                twin_banks[u].append(bank)
+            twins = sorted_twins[u] if u > 0 else twins_as_they_lie(unit_rows[u])
+            twin_banks[u] = [transpose_bank(twins[:, 2 * n : 2 * n + 2]) for n in range(PAIR)]
 
         def group_unit(u):
             grouped[u] = work.tile([P, UNIT_COLS * PACK], BF16, align_bytes=64, name="grouped")
-            words = grouped[u][:].bitcast(F32).rearrange("q (n a r u) -> q n a r u", n=PAIR, a=2, u=2)
-            nc.scalar.copy(out=words[:, 0], in_=twin_banks[u][0][:].rearrange("q a u r -> q a r u"))
-            copy = nc.scalar.copy if u % 2 or u < WEIGHT_UNITS else nc.vector.tensor_copy
-            copy(out=words[:, 1], in_=twin_banks[u][1][:].rearrange("q a u r -> q a r u"))
+            for n, copy in enumerate((nc.scalar.copy, nc.vector.tensor_copy if u % 2 else nc.scalar.copy)):
+                group_bank(twin_banks[u][n], grouped[u][:, n * BANK_VALUES : (n + 1) * BANK_VALUES], copy)
 
         def quantise_unit(u):
             if u not in unit_codes:
@@ -232,8 +225,7 @@ def tile_mla_pa_t_kernel(
         def copy_values(k):
             if k % PAIR == 0:
                 v_out[k // PAIR] = work.tile([P, PAIR, KEY_COLS], F32, name="v_out")
-            copy = nc.vector.tensor_copy if k % 4 == 3 else nc.scalar.copy
-            copy(out=v_out[k // PAIR][:, k % PAIR, :], in_=v_banks[k][:])
+            nc.scalar.copy(out=v_out[k // PAIR][:, k % PAIR, :], in_=v_banks[k][:])
             if k % PAIR == PAIR - 1:
                 nc.sync.dma_start(out=v_rows[k // PAIR], in_=v_out[k // PAIR][:])
 
@@ -244,11 +236,10 @@ def tile_mla_pa_t_kernel(
             )
 
         def multiply_keys(k):
-            if k % PAIR == 0:
-                products[k // PAIR] = work.tile([P, PAIR, HEADS, 2, HALF_D, 2], F32, name="products")
+            products[k] = work.tile([P, HEADS, 2, HALF_D, 2], F32, name="products", bufs=4)
             for h in range(HEADS):
                 nc.vector.scalar_tensor_tensor(
-                    out=products[k // PAIR][:, k % PAIR, h].rearrange("p w j e -> p w (j e)"),
+                    out=products[k][:, h].rearrange("p w j e -> p w (j e)"),
                     in0=k_banks[k][:, h].unsqueeze(1).to_broadcast([P, 2, D]),
                     scalar=rstd[k][:, h : h + 1],
                     in1=rope_table[:, k % SEQ_TILES].rearrange("p w j e -> p w (j e)"),
@@ -256,64 +247,89 @@ def tile_mla_pa_t_kernel(
                     op1=ALU.mult,
                 )
 
-        def sum_products(s, tiles, engine):
-            if tiles.start == 0:
-                k_out[s] = work.tile([P, PAIR, HEADS, HALF_D, 2], F32, name="k_out")
+        def sum_products(k):
+            s, n = divmod(k, PAIR)
+            if n == 0:
+                k_out[s] = work.tile([P, PAIR, KEY_COLS], F32, name="k_out")
+            engine = nc.vector if k == N_TILES - 1 else nc.gpsimd
             engine.tensor_tensor(
-                out=k_out[s][:, tiles].rearrange("p n h j e -> p (n h) j e"),
-                in0=products[s][:, tiles, :, 0].rearrange("p n h j e -> p (n h) j e"),
-                in1=products[s][:, tiles, :, 1].rearrange("p n h j e -> p (n h) j e")[:, :, :, ::-1],
+                out=k_out[s][:, n, :].rearrange("p (h j e) -> p h j e", h=HEADS, e=2),
+                in0=products[k][:, :, 0],
+                in1=products[k][:, :, 1, :, ::-1],
                 op=ALU.add,
             )
-            nc.sync.dma_start(
-                out=k_rows[s][:, tiles], in_=k_out[s][:, tiles].rearrange("p n h j e -> p n (h j e)")
+            if s == N_PAIRS - 1:
+                nc.sync.dma_start(out=k_rows[s][:, n, :], in_=k_out[s][:, n, :])
+            elif n == PAIR - 1:
+                nc.sync.dma_start(out=k_rows[s], in_=k_out[s][:])
+
+        wd_banks, wd_grouped = [], []
+
+        def quantise_wd(t):
+            columns = slice(t * C_PASSES * P, (t + 1) * C_PASSES * P)
+            nc.vector.quantize_mx(
+                out=wd_codes[:, columns].bitcast(FP8X4), scales=wd_scales[:, columns], in_=wd_grouped[t][:]
             )
 
-        for j in range(N_UNITS + 1):
-            if j < N_UNITS:
-                transpose_unit(j)
-            if AS_THEY_LIE <= j + 1 < N_UNITS:
-                sort_unit(j + 1)
-            if 0 <= j - 1:
-                group_unit(j - 1)
-            if 0 <= j - 2:
-                quantise_unit(j - 2)
-            if j - 3 in pair_of_unit:
-                latent_passes(j - 3)
-            if j - 4 in pair_of_unit:
-                group_latent(j - 4)
-            if j - 5 in pair_of_unit:
-                quantise_latent(j - 5)
+        for t in range(PACK):
+            wd_banks.append(transpose_bank(twins_as_they_lie(wd_sb[:, t, :])))
+        for t in range(PACK):
+            values = work.tile([P, BANK_VALUES], BF16, align_bytes=64, name="wd_values", bufs=PACK)
+            group_bank(wd_banks[t], values[:], nc.vector.tensor_copy if t % 2 else nc.scalar.copy)
+            wd_grouped.append(values)
+            if t == 1:
+                transpose_unit(0)
+                quantise_wd(0)
+        for t in range(1, PACK):
+            quantise_wd(t)
+        group_unit(0)
+        sort_unit(1)
+        quantise_unit(0)
+        transpose_unit(1)
+        sort_unit(2)
+        sort_unit(3)
+        group_unit(1)
+        latent_passes(0)
+
+        def if_pairs(stage, units):
+            for u in units:
+                if u in pair_of_unit:
+                    stage(u)
+
+        for j in range(2, N_UNITS, 2):
+            transpose_unit(j)
+            transpose_unit(j + 1)
+            for u in (j - 2, j - 1):
+                if u > 0:
+                    quantise_unit(u)
+            for u in (j + 2, j + 3):
+                if u < N_UNITS:
+                    sort_unit(u)
+            if j == 2:
+                group_latent(0)
+            group_unit(j)
+            group_unit(j + 1)
+            if j > 2:
+                if_pairs(latent_passes, (j - 2, j - 1))
+                if_pairs(group_latent, (j - 2, j - 1))
+                if_pairs(quantise_latent, (j - 4, j - 3))
+            else:
+                latent_passes(1)
+                group_latent(1)
 
         last = N_UNITS - 1
+        quantise_unit(last - 1)
         quantise_unit(last)
-        latent_passes(last - 1)
-        group_latent(last - 2)
-        quantise_latent(last - 3)
-        kv_passes(0)
-        kv_passes(1)
-        group_latent(last - 1)
-        quantise_latent(last - 2)
-        latent_passes(last)
-        sum_key_squares(0)
-        copy_values(0)
-        reciprocal_rms(0)
-        quantise_latent(last - 1)
-        multiply_keys(0)
-        group_latent(last)
-        quantise_latent(last)
+        for u in (last - 1, last):
+            latent_passes(u)
+            group_latent(u)
+        for u in range(last - 3, last + 1):
+            quantise_latent(u)
 
-        for k in range(1, N_TILES):
-            if k > 1:
-                kv_passes(k)
+        for k in range(N_TILES):
+            kv_passes(k)
             sum_key_squares(k)
             copy_values(k)
             reciprocal_rms(k)
             multiply_keys(k)
-            s = k // PAIR
-            if s < N_PAIRS - 1:
-                if k % PAIR == PAIR - 1:
-                    sum_products(s, slice(0, PAIR), nc.gpsimd)
-            else:
-                n = k % PAIR
-                sum_products(s, slice(n, n + 1), nc.gpsimd if n == 0 else nc.vector)
+            sum_products(k)

@@ -30,6 +30,7 @@ N_TILES = TOKENS // P
 SEQ_TILES = SEQ // P
 PAIR = 2
 N_PAIRS = N_TILES // PAIR
+SEQ_PAIRS = SEQ_TILES // PAIR
 UNIT_COLS = PAIR * 2 * P
 BANK_VALUES = 2 * P * PACK
 UP_UNITS = 2
@@ -46,32 +47,36 @@ def tile_mla_pa_t_kernel(
     tc, x, w_kv_down, w_kv_up, k_norm_w, freqs_cos, freqs_sin, out_0, out_1
 ):
     nc = tc.nc
-    x_rows = x.flatten_outer_dims().rearrange("(s p n) c -> s p n c", p=P, n=PAIR)
-    k_rows = out_0.rearrange("b t h d -> (b t) (h d)").rearrange("(s p n) f -> s p n f", p=P, n=PAIR)
-    v_rows = out_1.rearrange("b t h d -> (b t) (h d)").rearrange("(s p n) f -> s p n f", p=P, n=PAIR)
+    x_split = x.rearrange("b (p i n) c -> b i p n c", p=P, n=PAIR)
+    k_split = out_0.rearrange("b (p i n) h d -> b i p n (h d)", p=P, n=PAIR)
+    v_split = out_1.rearrange("b (p i n) h d -> b i p n (h d)", p=P, n=PAIR)
+    x_rows, k_rows, v_rows = (
+        [split[s // SEQ_PAIRS, s % SEQ_PAIRS] for s in range(N_PAIRS)] for split in (x_split, k_split, v_split)
+    )
 
     with ExitStack() as stack:
         stack.enter_context(tc.manual_schedule())
         const = stack.enter_context(tc.tile_pool(name="const", bufs=1))
         x_pool = stack.enter_context(tc.tile_pool(name="x", bufs=N_PAIRS))
         work = stack.enter_context(tc.tile_pool(name="work", bufs=3))
+        psum = stack.enter_context(tc.psum_pool(name="banks", bufs=4, reuse_waits="tile"))
 
         wd_sb = const.tile([P, PACK, C], BF16)
         wu_sb = const.tile([P, 2 * HEADS, R], BF16)
         cos_sb = const.tile([P, SEQ_TILES, HALF_D], BF16)
         sin_sb = const.tile([P, SEQ_TILES, HALF_D], BF16)
-        gain_sb = const.tile([P, HALF_D, 2], BF16)
+        gain_row = const.tile([P, D], BF16)
+        ones = const.tile([P, P], BF16)
+        nc.gpsimd.memset(gain_row[:], 0.0)
+        nc.gpsimd.memset(ones[:], 1.0)
 
         def load_table(table, source):
-            nc.sync.dma_start(
-                out=table[:].rearrange("p (s n) j -> p s n j", n=PAIR),
-                in_=source.rearrange("(s p n) j -> p s n j", p=P, n=PAIR),
-            )
+            nc.sync.dma_start(out=table[:], in_=source.rearrange("(p r) j -> p r j", r=SEQ_TILES))
 
         def load_wd(t):
             nc.sync.dma_start(out=wd_sb[:, t, :], in_=w_kv_down.rearrange("(p t) c -> p t c", t=PACK)[:, t, :])
 
-        nc.sync.dma_start(out=gain_sb[:].rearrange("p j e -> p (j e)"), in_=k_norm_w.partition_broadcast(P))
+        nc.sync.dma_start(out=gain_row[0:1, :], in_=k_norm_w.rearrange("(o d) -> o d", o=1))
         load_table(cos_sb, freqs_cos)
         load_wd(0)
         load_table(sin_sb, freqs_sin)
@@ -92,9 +97,14 @@ def tile_mla_pa_t_kernel(
         table_warmer = const.tile([P, 1], F32)
         nc.scalar.activation(out=table_warmer[:], in_=eps[:], func=ACT.Abs_reciprocal_sqrt)
 
+        gain_bank = psum.tile([P, HALF_D, 2], F32, tag="twins", name="gain_bank")
+        nc.tensor.matmul(
+            gain_bank[:].rearrange("p j e -> p (j e)"), lhsT=ones[:], rhs=gain_row[:], start=True, stop=True
+        )
+        gain_sb = const.tile([P, HALF_D, 2], F32)
         signed_gain = const.tile([P, HALF_D, 2], F32)
         rope_table = const.tile([P, SEQ_TILES, 2, HALF_D, 2], F32)
-
+        nc.vector.tensor_copy(out=gain_sb[:], in_=gain_bank[:])
         nc.vector.tensor_copy(out=signed_gain[:, :, 0], in_=gain_sb[:, :, 0])
         nc.vector.tensor_scalar_mul(out=signed_gain[:, :, 1], in0=gain_sb[:, :, 1], scalar1=-1.0)
         for row, angles, gain in ((0, cos_sb, gain_sb), (1, sin_sb, signed_gain)):
@@ -128,10 +138,9 @@ def tile_mla_pa_t_kernel(
         sorted_twins, twin_banks, grouped, latent_banks, latent_grouped = {}, {}, {}, {}, {}
         k_banks, v_banks, sum_squares, rstd, products, k_out, v_out = {}, {}, {}, {}, {}, {}, {}
 
-        psum = stack.enter_context(tc.psum_pool(name="banks", bufs=4, reuse_waits="tile"))
 
         def sort_unit(u):
-            twins = work.tile([P, 2 * PAIR, 2, P], F32, name="sorted_twins")
+            twins = work.tile([P, 2 * PAIR, 2, P], F32, name="sorted_twins", bufs=4)
             nc.vector.tensor_copy(out=twins[:], in_=twins_as_they_lie(unit_rows[u]))
             sorted_twins[u] = twins[:]
 
@@ -156,14 +165,14 @@ def tile_mla_pa_t_kernel(
             twin_banks[u] = [transpose_bank(twins[:, 2 * n : 2 * n + 2]) for n in range(PAIR)]
 
         def group_unit(u):
-            grouped[u] = work.tile([P, UNIT_COLS * PACK], BF16, align_bytes=64, name="grouped")
+            grouped[u] = work.tile([P, UNIT_COLS * PACK], BF16, align_bytes=64, name="grouped", bufs=4)
             for n, copy in enumerate((nc.scalar.copy, nc.vector.tensor_copy if u % 2 else nc.scalar.copy)):
                 group_bank(twin_banks[u][n], grouped[u][:, n * BANK_VALUES : (n + 1) * BANK_VALUES], copy)
 
         def quantise_unit(u):
             if u not in unit_codes:
-                x_codes = work.tile([P, UNIT_COLS], U32, align_bytes=64)
-                x_scales = work.tile([P, UNIT_COLS], U8, align_bytes=64)
+                x_codes = work.tile([P, UNIT_COLS], U32, align_bytes=64, bufs=4)
+                x_scales = work.tile([P, UNIT_COLS], U8, align_bytes=64, bufs=4)
                 unit_codes[u] = (x_codes[:], x_scales[:])
             codes, scales = unit_codes[u]
             nc.vector.quantize_mx(out=codes.bitcast(FP8X4), scales=scales, in_=grouped[u][:])
@@ -187,7 +196,7 @@ def tile_mla_pa_t_kernel(
                 latent_banks[u].append(bank)
 
         def group_latent(u):
-            latent_grouped[u] = work.tile([P, PAIR, P, PACK], BF16, align_bytes=64, name="latent_grouped")
+            latent_grouped[u] = work.tile([P, PAIR, P, PACK], BF16, align_bytes=64, name="latent_grouped", bufs=4)
             for n in range(PAIR):
                 nc.scalar.copy(out=latent_grouped[u][:, n], in_=latent_banks[u][n][:].rearrange("p t r -> p r t"))
 
@@ -320,13 +329,19 @@ def tile_mla_pa_t_kernel(
         last = N_UNITS - 1
         quantise_unit(last - 1)
         quantise_unit(last)
-        for u in (last - 1, last):
-            latent_passes(u)
-            group_latent(u)
+        latent_passes(last - 1)
+        group_latent(last - 1)
+        kv_passes(0)
+        sum_key_squares(0)
+        latent_passes(last)
+        group_latent(last)
+        copy_values(0)
+        reciprocal_rms(0)
         for u in range(last - 3, last + 1):
             quantise_latent(u)
-
-        for k in range(N_TILES):
+        multiply_keys(0)
+        sum_products(0)
+        for k in range(1, N_TILES):
             kv_passes(k)
             sum_key_squares(k)
             copy_values(k)

from contextlib import ExitStack

import concourse.mybir as mybir
from concourse.masks import make_identity

F32 = mybir.dt.float32
BF16 = mybir.dt.bfloat16
U32 = mybir.dt.uint32
U8 = mybir.dt.uint8
FP8X4 = mybir.dt.float8_e4m3fn_x4
ALU = mybir.AluOpType
ACT = mybir.ActivationFunctionType

P = 128
PACK = 4
K_PASS = P * PACK

TOKENS = 4 * 1024
SEQ = 1024
C = 1024
R = 512
HEADS = 4
D = 128
HALF_D = D // 2
KEY_COLS = HEADS * D
EPS = 1e-6

C_PASSES = C // K_PASS
N_TILES = TOKENS // P
SEQ_TILES = SEQ // P
PAIR = 2
N_PAIRS = N_TILES // PAIR
SEQ_PAIRS = SEQ_TILES // PAIR
UNIT_COLS = PAIR * 2 * P
BANK_VALUES = 2 * P * PACK
UP_UNITS = 2
PAIRS_BEFORE_UP = 8

FLOPS = 2 * TOKENS * C * R + 2 * TOKENS * R * 2 * KEY_COLS


def block(i):
    return slice(i * P, (i + 1) * P)


def tile_mla_pa_t_kernel(
    tc, x, w_kv_down, w_kv_up, k_norm_w, freqs_cos, freqs_sin, out_0, out_1
):
    nc = tc.nc
    x_split = x.rearrange("b (p i n) c -> b i p n c", p=P, n=PAIR)
    k_split = out_0.rearrange("b (p i n) h d -> b i p n (h d)", p=P, n=PAIR)
    v_split = out_1.rearrange("b (p i n) h d -> b i p n (h d)", p=P, n=PAIR)
    x_rows, k_rows, v_rows = (
        [split[s // SEQ_PAIRS, s % SEQ_PAIRS] for s in range(N_PAIRS)] for split in (x_split, k_split, v_split)
    )

    with ExitStack() as stack:
        stack.enter_context(tc.manual_schedule())
        const = stack.enter_context(tc.tile_pool(name="const", bufs=1))
        x_pool = stack.enter_context(tc.tile_pool(name="x", bufs=N_PAIRS))
        work = stack.enter_context(tc.tile_pool(name="work", bufs=3))
        psum = stack.enter_context(tc.psum_pool(name="banks", bufs=4, reuse_waits="tile"))

        wd_sb = const.tile([P, PACK, C], BF16)
        wu_sb = const.tile([P, 2 * HEADS, R], BF16)
        cos_sb = const.tile([P, SEQ_TILES, HALF_D], BF16)
        sin_sb = const.tile([P, SEQ_TILES, HALF_D], BF16)
        gain_row = const.tile([P, D], BF16)
        ones = const.tile([P, P], BF16)
        nc.gpsimd.memset(gain_row[:], 0.0)
        nc.gpsimd.memset(ones[:], 1.0)

        def load_table(table, source):
            nc.sync.dma_start(out=table[:], in_=source.rearrange("(p r) j -> p r j", r=SEQ_TILES))

        def load_wd(t):
            nc.sync.dma_start(out=wd_sb[:, t, :], in_=w_kv_down.rearrange("(p t) c -> p t c", t=PACK)[:, t, :])

        nc.sync.dma_start(out=gain_row[0:1, :], in_=k_norm_w.rearrange("(o d) -> o d", o=1))
        load_table(cos_sb, freqs_cos)
        load_wd(0)
        load_table(sin_sb, freqs_sin)
        for t in range(1, PACK):
            load_wd(t)
        x_sb = []
        for s in range(N_PAIRS):
            if s == PAIRS_BEFORE_UP:
                nc.sync.dma_start(out=wu_sb[:], in_=w_kv_up.rearrange("(b p) r -> p b r", p=P))
            x_pair = x_pool.tile([P, PAIR, C], BF16)
            nc.sync.dma_start(out=x_pair[:], in_=x_rows[s])
            x_sb.append(x_pair)

        identity = const.tile([P, P], F32)
        make_identity(nc, identity[:])
        eps = const.tile([P, 1], F32)
        nc.vector.memset(eps[:], EPS)
        table_warmer = const.tile([P, 1], F32)
        nc.scalar.activation(out=table_warmer[:], in_=eps[:], func=ACT.Abs_reciprocal_sqrt)

        gain_bank = psum.tile([P, HALF_D, 2], F32, tag="twins", name="gain_bank")
        nc.tensor.matmul(
            gain_bank[:].rearrange("p j e -> p (j e)"), lhsT=ones[:], rhs=gain_row[:], start=True, stop=True
        )
        gain_sb = const.tile([P, HALF_D, 2], F32)
        signed_gain = const.tile([P, HALF_D, 2], F32)
        rope_table = const.tile([P, SEQ_TILES, 2, HALF_D, 2], F32)
        nc.vector.tensor_copy(out=gain_sb[:], in_=gain_bank[:])
        nc.vector.tensor_copy(out=signed_gain[:, :, 0], in_=gain_sb[:, :, 0])
        nc.vector.tensor_scalar_mul(out=signed_gain[:, :, 1], in0=gain_sb[:, :, 1], scalar1=-1.0)
        for row, angles, gain in ((0, cos_sb, gain_sb), (1, sin_sb, signed_gain)):
            nc.vector.tensor_tensor(
                out=rope_table[:, :, row],
                in0=angles[:].unsqueeze(3).to_broadcast([P, SEQ_TILES, HALF_D, 2]),
                in1=gain[:].unsqueeze(1).to_broadcast([P, SEQ_TILES, HALF_D, 2]),
                op=ALU.mult,
            )

        wd_codes = const.tile([P, UP_UNITS * UNIT_COLS], U32, align_bytes=64)
        wd_scales = const.tile([P, UP_UNITS * UNIT_COLS], U8, align_bytes=64)
        wu_codes = const.tile([P, UP_UNITS * UNIT_COLS], U32, align_bytes=64)
        wu_scales = const.tile([P, UP_UNITS * UNIT_COLS], U8, align_bytes=64)
        latent_codes = const.tile([P, N_TILES * P], U32, align_bytes=64)
        latent_scales = const.tile([P, N_TILES * P], U8, align_bytes=64)

        unit_rows = []
        unit_codes = {}
        pair_of_unit = {}
        for s in range(N_PAIRS):
            if s == PAIRS_BEFORE_UP:
                for i in range(UP_UNITS):
                    columns = slice(i * UNIT_COLS, (i + 1) * UNIT_COLS)
                    unit_codes[len(unit_rows)] = (wu_codes[:, columns], wu_scales[:, columns])
                    unit_rows.append(wu_sb[:, 4 * i : 4 * (i + 1), :].rearrange("p b r -> p (b r)"))
            pair_of_unit[len(unit_rows)] = s
            unit_rows.append(x_sb[s][:].rearrange("p n c -> p (n c)"))
        N_UNITS = len(unit_rows)

        sorted_twins, twin_banks, grouped, latent_banks, latent_grouped = {}, {}, {}, {}, {}
        k_banks, v_banks, sum_squares, rstd, products, k_out, v_out = {}, {}, {}, {}, {}, {}, {}


        def sort_unit(u):
            twins = work.tile([P, 2 * PAIR, 2, P], F32, name="sorted_twins", bufs=4)
            nc.vector.tensor_copy(out=twins[:], in_=twins_as_they_lie(unit_rows[u]))
            sorted_twins[u] = twins[:]

        def transpose_bank(groups):
            bank = psum.tile([P, 2, 2, P], F32, tag="twins", name="twin_bank")
            for a in range(2):
                for half in range(2):
                    nc.tensor.transpose(bank[:, a, half, :], groups[:, a, half, :], identity[:])
            return bank

        def group_bank(bank, values, copy):
            copy(
                out=values.bitcast(F32).rearrange("q (a r u) -> q a r u", a=2, u=2),
                in_=bank[:].rearrange("q a u r -> q a r u"),
            )

        def twins_as_they_lie(rows):
            return rows.bitcast(F32).rearrange("p (g q u) -> p g u q", q=P, u=2)

        def transpose_unit(u):
            twins = sorted_twins[u] if u > 0 else twins_as_they_lie(unit_rows[u])
            twin_banks[u] = [transpose_bank(twins[:, 2 * n : 2 * n + 2]) for n in range(PAIR)]

        def group_unit(u):
            grouped[u] = work.tile([P, UNIT_COLS * PACK], BF16, align_bytes=64, name="grouped", bufs=4)
            for n, copy in enumerate((nc.scalar.copy, nc.vector.tensor_copy if u % 2 else nc.scalar.copy)):
                group_bank(twin_banks[u][n], grouped[u][:, n * BANK_VALUES : (n + 1) * BANK_VALUES], copy)

        def quantise_unit(u):
            if u not in unit_codes:
                x_codes = work.tile([P, UNIT_COLS], U32, align_bytes=64, bufs=4)
                x_scales = work.tile([P, UNIT_COLS], U8, align_bytes=64, bufs=4)
                unit_codes[u] = (x_codes[:], x_scales[:])
            codes, scales = unit_codes[u]
            nc.vector.quantize_mx(out=codes.bitcast(FP8X4), scales=scales, in_=grouped[u][:])

        def latent_passes(u):
            x_codes, x_scales = unit_codes[u]
            latent_banks[u] = []
            for n in range(PAIR):
                bank = psum.tile([P, PACK, P], F32, tag="latent", name="latent_bank")
                for t in range(PACK):
                    for g in range(C_PASSES):
                        nc.tensor.matmul_mx(
                            out=bank[:, t, :],
                            lhsT=wd_codes[:, block(t * C_PASSES + g)].bitcast(FP8X4),
                            lhsT_scale=wd_scales[:, block(t * C_PASSES + g)],
                            rhs=x_codes[:, block(n * C_PASSES + g)].bitcast(FP8X4),
                            rhs_scale=x_scales[:, block(n * C_PASSES + g)],
                            start=(g == 0),
                            stop=(g == C_PASSES - 1),
                        )
                latent_banks[u].append(bank)

        def group_latent(u):
            latent_grouped[u] = work.tile([P, PAIR, P, PACK], BF16, align_bytes=64, name="latent_grouped", bufs=4)
            for n in range(PAIR):
                nc.scalar.copy(out=latent_grouped[u][:, n], in_=latent_banks[u][n][:].rearrange("p t r -> p r t"))

        def quantise_latent(u):
            s = pair_of_unit[u]
            columns = slice(s * PAIR * P, (s + 1) * PAIR * P)
            nc.vector.quantize_mx(
                out=latent_codes[:, columns].bitcast(FP8X4),
                scales=latent_scales[:, columns],
                in_=latent_grouped[u][:].rearrange("p n r t -> p (n r t)"),
            )

        def kv_passes(k):
            k_banks[k] = psum.tile([P, HEADS, D], F32, tag="twins", name="k_bank")
            v_banks[k] = psum.tile([P, KEY_COLS], F32, tag="latent", name="v_bank")
            for bank, first_col in ((k_banks[k][:].rearrange("p h d -> p (h d)"), 0), (v_banks[k][:], KEY_COLS)):
                nc.tensor.matmul_mx(
                    out=bank,
                    lhsT=latent_codes[:, block(k)].bitcast(FP8X4),
                    lhsT_scale=latent_scales[:, block(k)],
                    rhs=wu_codes[:, first_col : first_col + KEY_COLS].bitcast(FP8X4),
                    rhs_scale=wu_scales[:, first_col : first_col + KEY_COLS],
                    start=True,
                    stop=True,
                )

        def sum_key_squares(k):
            squares = work.tile([P, HEADS, D], F32)
            sum_squares[k] = work.tile([P, HEADS], F32, name="sum_squares")
            for h in range(HEADS):
                nc.scalar.activation(
                    out=squares[:, h], in_=k_banks[k][:, h], func=ACT.Square, accum_out=sum_squares[k][:, h : h + 1]
                )

        def copy_values(k):
            if k % PAIR == 0:
                v_out[k // PAIR] = work.tile([P, PAIR, KEY_COLS], F32, name="v_out")
            nc.scalar.copy(out=v_out[k // PAIR][:, k % PAIR, :], in_=v_banks[k][:])
            if k % PAIR == PAIR - 1:
                nc.sync.dma_start(out=v_rows[k // PAIR], in_=v_out[k // PAIR][:])

        def reciprocal_rms(k):
            rstd[k] = work.tile([P, HEADS], F32, name="rstd")
            nc.scalar.activation(
                out=rstd[k][:], in_=sum_squares[k][:], func=ACT.Abs_reciprocal_sqrt, scale=1.0 / D, bias=eps[:]
            )

        def multiply_keys(k):
            products[k] = work.tile([P, HEADS, 2, HALF_D, 2], F32, name="products", bufs=4)
            for h in range(HEADS):
                nc.vector.scalar_tensor_tensor(
                    out=products[k][:, h].rearrange("p w j e -> p w (j e)"),
                    in0=k_banks[k][:, h].unsqueeze(1).to_broadcast([P, 2, D]),
                    scalar=rstd[k][:, h : h + 1],
                    in1=rope_table[:, k % SEQ_TILES].rearrange("p w j e -> p w (j e)"),
                    op0=ALU.mult,
                    op1=ALU.mult,
                )

        def sum_products(k):
            s, n = divmod(k, PAIR)
            if n == 0:
                k_out[s] = work.tile([P, PAIR, KEY_COLS], F32, name="k_out")
            engine = nc.vector if k == N_TILES - 1 else nc.gpsimd
            engine.tensor_tensor(
                out=k_out[s][:, n, :].rearrange("p (h j e) -> p h j e", h=HEADS, e=2),
                in0=products[k][:, :, 0],
                in1=products[k][:, :, 1, :, ::-1],
                op=ALU.add,
            )
            if s == N_PAIRS - 1:
                nc.sync.dma_start(out=k_rows[s][:, n, :], in_=k_out[s][:, n, :])
            elif n == PAIR - 1:
                nc.sync.dma_start(out=k_rows[s], in_=k_out[s][:])

        wd_banks, wd_grouped = [], []

        def quantise_wd(t):
            columns = slice(t * C_PASSES * P, (t + 1) * C_PASSES * P)
            nc.vector.quantize_mx(
                out=wd_codes[:, columns].bitcast(FP8X4), scales=wd_scales[:, columns], in_=wd_grouped[t][:]
            )

        for t in range(PACK):
            wd_banks.append(transpose_bank(twins_as_they_lie(wd_sb[:, t, :])))
        for t in range(PACK):
            values = work.tile([P, BANK_VALUES], BF16, align_bytes=64, name="wd_values", bufs=PACK)
            group_bank(wd_banks[t], values[:], nc.vector.tensor_copy if t % 2 else nc.scalar.copy)
            wd_grouped.append(values)
            if t == 1:
                transpose_unit(0)
                quantise_wd(0)
        for t in range(1, PACK):
            quantise_wd(t)
        group_unit(0)
        sort_unit(1)
        quantise_unit(0)
        transpose_unit(1)
        sort_unit(2)
        sort_unit(3)
        group_unit(1)
        latent_passes(0)

        def if_pairs(stage, units):
            for u in units:
                if u in pair_of_unit:
                    stage(u)

        for j in range(2, N_UNITS, 2):
            transpose_unit(j)
            transpose_unit(j + 1)
            for u in (j - 2, j - 1):
                if u > 0:
                    quantise_unit(u)
            for u in (j + 2, j + 3):
                if u < N_UNITS:
                    sort_unit(u)
            if j == 2:
                group_latent(0)
            group_unit(j)
            group_unit(j + 1)
            if j > 2:
                if_pairs(latent_passes, (j - 2, j - 1))
                if_pairs(group_latent, (j - 2, j - 1))
                if_pairs(quantise_latent, (j - 4, j - 3))
            else:
                latent_passes(1)
                group_latent(1)

        last = N_UNITS - 1
        quantise_unit(last - 1)
        quantise_unit(last)
        latent_passes(last - 1)
        group_latent(last - 1)
        kv_passes(0)
        sum_key_squares(0)
        latent_passes(last)
        group_latent(last)
        copy_values(0)
        reciprocal_rms(0)
        for u in range(last - 3, last + 1):
            quantise_latent(u)
        multiply_keys(0)
        sum_products(0)
        for k in range(1, N_TILES):
            kv_passes(k)
            sum_key_squares(k)
            copy_values(k)
            reciprocal_rms(k)
            multiply_keys(k)
            sum_products(k)
